import numpy as np
import ml_dtypes


def mxq(x, axis, fmt="e4m3"):
    dtype, down = {"e4m3": (ml_dtypes.float8_e4m3fn, 7), "e5m2": (ml_dtypes.float8_e5m2, 14)}[fmt]
    v = np.moveaxis(np.asarray(x, np.float32).astype(ml_dtypes.bfloat16).astype(np.float64), axis, -1)
    blocks = v.reshape(v.shape[:-1] + (-1, 32))
    amax = np.abs(blocks).max(-1, keepdims=True)
    byte = np.maximum(np.where(amax > 0, np.frexp(amax)[1] - 1 + 127, 0) - down, 1)
    scale = np.exp2(byte - 127.0)
    codes = (blocks / scale).astype(np.float32).astype(dtype).astype(np.float64)
    return np.moveaxis((codes * scale).reshape(v.shape), -1, axis)


WIDE = False


def mx_kscale(k):
    if not WIDE:
        return np.ones(k)
    levels = np.array([18, -18])
    if k % 512:
        return np.exp2(np.random.permutation(np.resize(levels, k // 32))).repeat(32)
    a = np.empty((k // 512, 16))
    for p in range(k // 512):
        a[p, :8] = np.random.permutation(np.resize(levels, 8))
        for g in range(8):
            far = levels[np.abs(levels - a[p, g]) >= 10]
            a[p, g + 8] = far[np.random.randint(len(far))]
    return np.exp2(a.ravel()).repeat(32)


BF16 = ml_dtypes.bfloat16


def bf(x):
    return np.asarray(x, np.float32).astype(BF16)


def f64(x):
    return np.asarray(x).astype(np.float64)


B, N, F, D = 1, 2048, 512, 512


def degree_factor(adj):
    d = np.sum(adj, axis=-1)
    with np.errstate(divide="ignore"):
        r = np.power(d, -0.5)
    return np.where(np.isinf(r), 0.0, r)


def pre_relu(inputs, adj, r, W_kernel, W_bias):
    feats = inputs @ W_kernel + W_bias
    return r[..., :, None] * (adj @ (r[..., :, None] * feats))


def setup_inputs():
    u = mx_kscale(N)
    v = mx_kscale(D)
    s = mx_kscale(N)
    a = np.exp2(np.random.uniform(-2.0, 2.0, size=(B, N, 1)))
    x0 = bf(np.random.standard_normal((B, N, F)))
    adj0 = bf(np.random.uniform(size=(B, N, N)) * a)
    w0 = bf(np.random.standard_normal((F, D)) * 0.2 * np.sqrt(N / F))
    b0 = bf(np.random.standard_normal(D) * 0.2)
    r = degree_factor(f64(adj0))
    z2 = pre_relu(f64(x0), f64(adj0), r, f64(w0), f64(b0))
    g = np.random.standard_normal((B, N, D)) * np.exp2(np.random.randint(-6, 1, (B, N, 1))) * 16.0
    g = g * (np.abs(z2) > 1e-4)
    return {"inputs": bf(f64(x0) * s[:, None]),
            "adj": bf(f64(adj0) / u[:, None] / s),
            "W_kernel": bf(f64(w0) / v),
            "W_bias": b0,
            "r": np.asarray(r, np.float32),
            "z2": np.asarray(z2, np.float32),
            "grad_out": bf(g * u[:, None] * v)}


def reference(inputs, adj, W_kernel, W_bias, r, z2, grad_out):
    rf = f64(r)[:, :, None]
    dz2 = np.where(f64(z2) > 0.0, f64(grad_out), 0.0) * rf
    dh = np.swapaxes(mxq(f64(adj), 1, "e4m3"), 1, 2) @ mxq(dz2, 1, "e5m2")
    dz1 = (dh * rf).reshape(B * N, D)
    dx = mxq(dz1, 1, "e5m2") @ mxq(f64(W_kernel), 1, "e4m3").T
    x = f64(inputs).reshape(B * N, F)
    dw = mxq(x, 0, "e4m3").T @ mxq(dz1, 0, "e5m2")
    return dx.reshape(B, N, F), dw

@@ -1,0 +1,325 @@
+from contextlib import ExitStack
+
+import concourse.mybir as mybir
+from concourse.masks import make_identity
+
+NODES, F_IN, D_OUT = 2048, 512, 512
+FLOPS = 2 * NODES * NODES * D_OUT + 2 * 2 * NODES * F_IN * D_OUT
+BYTES = 2 * (NODES * F_IN + NODES * NODES + F_IN * D_OUT + NODES * D_OUT) + 4 * (NODES + NODES * D_OUT) + 4 * (NODES * F_IN + F_IN * D_OUT)
+
+F32 = mybir.dt.float32
+BF16 = mybir.dt.bfloat16
+U32 = mybir.dt.uint32
+U8 = mybir.dt.uint8
+E4M3 = mybir.dt.float8_e4m3fn_x4
+E5M2 = mybir.dt.float8_e5m2_x4
+ALU = mybir.AluOpType
+COPY = mybir.ActivationFunctionType.Copy
+
+P = 128
+PACK = 4
+GROUP = P * PACK
+GROUPS = NODES // GROUP
+HALF = NODES // 2
+STEP = 4
+
+
+def tile_gcn_v_kernel(tc, inputs, adj, W_kernel, W_bias, r, z2, grad_out, out_0, out_1):
+    nc = tc.nc
+    x_rows = inputs.rearrange("o (g p j) f -> g p (o j) f", g=GROUPS, j=PACK)
+    adj_rows = adj.rearrange("o (g p j) m -> g p (o j) m", g=GROUPS, j=PACK)
+    z2_rows = z2.rearrange("o (g p j) w -> g p (o j) w", g=GROUPS, j=PACK)
+    grad_rows = grad_out.rearrange("o (g p j) w -> g p (o j) w", g=GROUPS, j=PACK)
+    r_cols = r.rearrange("o (g p j) -> p (o g) j", g=GROUPS, j=PACK)
+    w_rows = W_kernel.rearrange("(a p) j -> p a j", p=P)
+    dx_rows = out_0.rearrange("o (g p j) f -> g p (o j) f", g=GROUPS, j=PACK)
+
+    with ExitStack() as ctx:
+        keep = ctx.enter_context(tc.tile_pool(name="keep", bufs=1))
+        codes = ctx.enter_context(tc.tile_pool(name="codes", bufs=1))
+        stage = ctx.enter_context(tc.tile_pool(name="stage", bufs=3))
+        psum = ctx.enter_context(tc.psum_pool(name="psum", bufs=1))
+
+        def bank(i):
+            return psum.tile([P, 512], F32, name=f"bank{i}")
+
+        def operand(name, bufs):
+            return (codes.tile([P, GROUP], U32, name=f"{name}_codes", bufs=bufs, align_bytes=64),
+                    codes.tile([P, GROUP], U8, name=f"{name}_scales", bufs=bufs, align_bytes=64))
+
+        ident = keep.tile([P, P], F32, name="ident")
+        make_identity(nc, ident[:])
+        r_sb = keep.tile([P, GROUPS, PACK], F32, name="r_sb")
+        nc.scalar.dma_start(out=r_sb[:], in_=r_cols)
+        adj_raw, z2_raw, grad_raw, x_raw = {}, {}, {}, {}
+
+        def load_z2(g):
+            z2_raw[g] = stage.tile([P, PACK, D_OUT], F32, name="z2_raw")
+            nc.sync.dma_start(out=z2_raw[g][:], in_=z2_rows[g])
+
+        def load_grad(g):
+            grad_raw[g] = stage.tile([P, PACK, D_OUT], BF16, name="grad_raw", tag="rows", bufs=4)
+            nc.sync.dma_start(out=grad_raw[g][:], in_=grad_rows[g])
+
+        def load_adj(g, G, width):
+            raw = stage.tile([P, PACK, width * GROUP], BF16, name=f"adj_raw{width}", bufs=6 if width == 1 else 4)
+            nc.sync.dma_start(out=raw[:], in_=adj_rows[g][:, :, G * GROUP : (G + width) * GROUP])
+            for k in range(width):
+                adj_raw[g, G + k] = raw[:, :, k * GROUP : (k + 1) * GROUP]
+
+        def load_x(g):
+            x_raw[g] = stage.tile([P, PACK, F_IN], BF16, name="x_raw", tag="rows", bufs=4)
+            nc.sync.dma_start(out=x_raw[g][:], in_=x_rows[g])
+
+        load_adj(0, 0, 1)
+        load_adj(1, 0, 1)
+        for g in range(GROUPS):
+            load_grad(g)
+            if g > 1:
+                load_adj(g, 0, 1)
+            load_z2(g)
+        load_adj(0, 1, 1)
+        load_adj(1, 1, 1)
+        w_raw = keep.tile([P, 4, D_OUT], BF16, name="w_raw")
+        nc.sync.dma_start(out=w_raw[:], in_=w_rows)
+        load_adj(2, 1, 1)
+        load_adj(3, 1, 1)
+        load_x(0)
+        load_adj(0, 2, 2)
+        load_adj(1, 2, 2)
+        load_x(1)
+        load_adj(2, 2, 2)
+        load_adj(3, 2, 2)
+        load_x(2)
+        load_x(3)
+
+        def copy(engine, out, in_):
+            if engine == "V":
+                nc.vector.tensor_copy(out=out, in_=in_)
+            else:
+                nc.scalar.copy(out=out, in_=in_)
+
+        def quantize(laid, name, fmt, bufs=4):
+            words, scales = operand(name, bufs)
+            nc.vector.quantize_mx(out=words[:].bitcast(fmt), scales=scales[:], in_=laid[:])
+            return words, scales
+
+        def laid_tile(name):
+            return stage.tile([P, GROUP * PACK], BF16, name=name, tag="laid", bufs=8, align_bytes=64)
+
+        def lay_rows(engine, rows, laid):
+            copy(engine, laid.rearrange("p (c i j) -> p c j i", i=STEP, j=PACK), rows.rearrange("p j (c i) -> p c j i", i=STEP))
+
+        gr, dz2_laid, dz2_q, adj_laid, adj_q = {}, {}, {}, {}, {}
+
+        def dz2_scale(g):
+            gr[g] = stage.tile([P, PACK, D_OUT], F32, name="gr", tag="f32", bufs=3)
+            for j in range(PACK):
+                nc.scalar.activation(out=gr[g][:, j, :], in_=grad_raw[g][:, j, :], func=COPY, scale=r_sb[:, g, j : j + 1])
+
+        def dz2_mask(g):
+            dz2_laid[g] = laid_tile("dz2_laid")
+            nc.vector.scalar_tensor_tensor(
+                out=dz2_laid[g][:].rearrange("p (w j) -> p w j", j=PACK),
+                in0=z2_raw[g][:].rearrange("p j w -> p w j"), scalar=0.0,
+                in1=gr[g][:].rearrange("p j w -> p w j"), op0=ALU.is_gt, op1=ALU.mult)
+
+        def dz2_quant(g):
+            dz2_q[g] = quantize(dz2_laid[g], "dz2", E5M2)
+
+        def adj_lay(g, G, engine):
+            adj_laid[g, G] = laid_tile("adj_laid")
+            copy(engine, adj_laid[g, G][:].rearrange("p (t q j) -> p t q j", t=PACK, j=PACK), adj_raw[g, G].rearrange("p j (q t) -> p t q j", t=PACK))
+
+        def adj_quant(g, G):
+            adj_q[g, G] = quantize(adj_laid[g, G], "adj", E4M3, 8)
+
+        w_bank, w_q = {}, {}
+
+        def w_turn(b):
+            words = w_raw[:].rearrange("p a w -> p (a w)").bitcast(F32)
+            w_bank[b] = bank(4 + b)
+            for k in range(4):
+                w0 = 512 * b + 256 * (k // 2) + k % 2
+                nc.tensor.transpose(w_bank[b][:, P * k : P * (k + 1)], words[:, w0 : w0 + 255 : 2], ident[:])
+
+        def w_out(b, engine):
+            if b == 0:
+                w_bank["laid"] = laid_tile("w_laid")
+            words = w_bank["laid"][:].bitcast(F32)[:, 512 * b : 512 * (b + 1)]
+            copy(engine, words.rearrange("p (a f u) -> p a f u", a=2, u=2), w_bank[b][:].rearrange("p (a u f) -> p a f u", a=2, u=2))
+
+        def w_quant():
+            w_q[0], w_q[1] = quantize(w_bank["laid"], "w", E4M3, 1)
+
+        dh = {}
+
+        def dh_pass(g, G):
+            for t in range(PACK):
+                if g == 0:
+                    dh[G, t] = bank(4 * (G % 2) + t)
+                cols = slice(P * t, P * (t + 1))
+                nc.tensor.matmul_mx(
+                    out=dh[G, t][:], lhsT=adj_q[g, G][0][:, cols].bitcast(E4M3), lhsT_scale=adj_q[g, G][1][:, cols],
+                    rhs=dz2_q[g][0][:].bitcast(E5M2), rhs_scale=dz2_q[g][1][:], start=(g == 0), stop=(g == GROUPS - 1))
+
+        dz1, dz1_f, dz1_laid, dz1_fq, dz1_mq, turned = {}, {}, {}, {}, {}, {}
+
+        def dz1_tile(G):
+            dz1[G] = stage.tile([P, PACK, D_OUT], BF16, name="dz1", bufs=2)
+
+        def dh_out(G, t, engine):
+            out = dz1[G][:, t, :].rearrange("p (u q e) -> p u q e", u=2, e=2)
+            in_ = dh[G, t][:].rearrange("p (q u e) -> p u q e", u=2, e=2)
+            if engine == "V":
+                nc.vector.tensor_scalar(out=out, in0=in_, scalar1=r_sb[:, G, t : t + 1], scalar2=None, op0=ALU.mult)
+            else:
+                nc.scalar.activation(out=out, in_=in_, func=COPY, scale=r_sb[:, G, t : t + 1])
+
+        def turn(G, b):
+            words = dz1[G][:].rearrange("p t w -> p (t w)").bitcast(F32)
+            turned[G, b] = bank(4 * (G % 2) + b)
+            for k in range(4):
+                w0 = 512 * b + P * k
+                nc.tensor.transpose(turned[G, b][:, P * k : P * (k + 1)], words[:, w0 : w0 + P], ident[:])
+
+        def turn_out(G, b, engine):
+            if b == 0:
+                dz1_f[G] = laid_tile("dz1_f")
+            words = dz1_f[G][:].bitcast(F32)[:, 512 * b : 512 * (b + 1)]
+            copy(engine, words.rearrange("p (t m u) -> p t m u", t=2, u=2), turned[G, b][:].rearrange("p (t u m) -> p t m u", t=2, u=2))
+
+        def dz1_lay(G, engine):
+            dz1_laid[G] = laid_tile("dz1_laid")
+            lay_rows(engine, dz1[G][:], dz1_laid[G][:])
+
+        def dz1_quant_f(G):
+            dz1_fq[G] = quantize(dz1_f[G], "dz1_f", E5M2, 2)
+
+        def dz1_quant_m(G):
+            dz1_mq[G] = quantize(dz1_laid[G], "dz1_m", E5M2)
+
+        dx, dx_sb = {}, {}
+
+        def dx_pass(G, t):
+            dx[G, t] = bank(4 * (G % 2) + (2 + t) % 4)
+            cols = slice(P * t, P * (t + 1))
+            nc.tensor.matmul_mx(
+                out=dx[G, t][:], lhsT=dz1_fq[G][0][:, cols].bitcast(E5M2), lhsT_scale=dz1_fq[G][1][:, cols],
+                rhs=w_q[0][:].bitcast(E4M3), rhs_scale=w_q[1][:], start=True, stop=True)
+
+        def dx_out(G, t, engine):
+            if t == 0:
+                dx_sb[G] = stage.tile([P, PACK, F_IN], F32, name="dx_sb", tag="f32", bufs=3)
+            copy(engine, dx_sb[G][:, t, :], dx[G, t][:])
+            if G == GROUPS - 1:
+                nc.sync.dma_start(out=dx_rows[G][:, t, :], in_=dx_sb[G][:, t, :])
+            elif t % 2 == 1:
+                nc.sync.dma_start(out=dx_rows[G][:, t - 1 : t + 1, :], in_=dx_sb[G][:, t - 1 : t + 1, :])
+
+        x_laid, x_q = {}, {}
+
+        def x_lay(G, engine, c0=0, c1=F_IN):
+            if c0 == 0:
+                x_laid[G] = laid_tile("x_laid")
+            lay_rows(engine, x_raw[G][:, :, c0:c1], x_laid[G][:, PACK * c0 : PACK * c1])
+
+        def x_quant(G):
+            x_q[G] = quantize(x_laid[G], "x", E4M3)
+
+        dw, dw_sb = {}, {}
+
+        def dw_pass(G, a):
+            if G == 0:
+                dw[a] = bank((2 + a) % 4)
+            cols = slice(P * a, P * (a + 1))
+            nc.tensor.matmul_mx(
+                out=dw[a][:], lhsT=x_q[G][0][:, cols].bitcast(E4M3), lhsT_scale=x_q[G][1][:, cols],
+                rhs=dz1_mq[G][0][:].bitcast(E5M2), rhs_scale=dz1_mq[G][1][:], start=(G == 0), stop=(G == GROUPS - 1))
+
+        def dw_out(a, engine):
+            if a == 0:
+                dw_sb[0] = stage.tile([P, F_IN // P, D_OUT], F32, name="dw_sb", tag="f32", bufs=3)
+            copy(engine, dw_sb[0][:, a, :].rearrange("p (q u e) -> p q u e", u=2, e=2), dw[a][:].rearrange("p (u q e) -> p q u e", u=2, e=2))
+            nc.sync.dma_start(out=out_1[P * a : P * (a + 1), :], in_=dw_sb[0][:, a, :])
+
+        with tc.manual_schedule():
+            adj_lay(0, 0, "V")
+            adj_lay(1, 0, "V")
+            adj_quant(0, 0)
+            adj_quant(1, 0)
+            for g in range(GROUPS):
+                dz2_scale(g)
+                if g > 1:
+                    adj_lay(g, 0, "S")
+                dz2_mask(g)
+                if g > 1:
+                    adj_quant(g, 0)
+                dz2_quant(g)
+                dh_pass(g, 0)
+            adj_lay(0, 1, "S")
+            w_turn(0)
+            w_turn(1)
+            for G in range(GROUPS - 1):
+                dz1_tile(G)
+                for t in range(PACK):
+                    dh_out(G, t, "S")
+                if G > 0:
+                    adj_lay(0, G + 1, "V")
+                adj_lay(1, G + 1, "V")
+                adj_quant(0, G + 1)
+                for b in range(2):
+                    turn(G, b)
+                if G == 0:
+                    for b in range(2):
+                        w_out(b, "S")
+                if G > 0:
+                    x_lay(G, "S", 0, 256)
+                adj_lay(2, G + 1, "V")
+                dh_pass(0, G + 1)
+                adj_quant(1, G + 1)
+                dz1_lay(G, "V")
+                for b in range(2):
+                    turn_out(G, b, "S")
+                adj_lay(3, G + 1, "S")
+                dh_pass(1, G + 1)
+                if G == 0:
+                    w_quant()
+                dz1_quant_f(G)
+                for t in range(PACK):
+                    dx_pass(G, t)
+                if G == 0:
+                    x_lay(G, "S", 0, 256)
+                x_lay(G, "V", 256, 512)
+                for g in range(2, PACK):
+                    adj_quant(g, G + 1)
+                    dh_pass(g, G + 1)
+                dz1_quant_m(G)
+                for t in range(PACK):
+                    dx_out(G, t, "S")
+                x_quant(G)
+            x_lay(3, "V")
+            x_quant(3)
+            dz1_tile(3)
+            for t in range(PACK):
+                dh_out(3, t, "SSVV"[t])
+            for k in range(2):
+                for a in range(4):
+                    dw_pass(k, a)
+            for b in range(2):
+                turn(3, b)
+            for a in range(4):
+                dw_pass(2, a)
+            for b in range(2):
+                turn_out(3, b, "SV"[b])
+            dz1_quant_f(3)
+            for t in range(PACK):
+                dx_pass(3, t)
+            dz1_lay(3, "V")
+            dz1_quant_m(3)
+            for t in range(PACK):
+                dx_out(3, t, "S")
+            for a in range(4):
+                dw_pass(3, a)
+            for a in range(4):
+                dw_out(a, "VS"[a % 2])

@@ -71,13 +71,12 @@ def tile_gcn_v_kernel(tc, inputs, adj, W_kernel, W_bias, r, z2, grad_out, out_0,
             x_raw[g] = stage.tile([P, PACK, F_IN], BF16, name="x_raw", tag="rows", bufs=4)
             nc.sync.dma_start(out=x_raw[g][:], in_=x_rows[g])
 
-        load_adj(0, 0, 1)
-        load_adj(1, 0, 1)
         for g in range(GROUPS):
-            load_grad(g)
-            if g > 1:
-                load_adj(g, 0, 1)
             load_z2(g)
+            if g < 3:
+                load_grad(g)
+            load_adj(g, 0, 1)
+        load_grad(3)
         load_adj(0, 1, 1)
         load_adj(1, 1, 1)
         w_raw = keep.tile([P, 4, D_OUT], BF16, name="w_raw")
@@ -110,26 +109,26 @@ def tile_gcn_v_kernel(tc, inputs, adj, W_kernel, W_bias, r, z2, grad_out, out_0,
         def lay_rows(engine, rows, laid):
             copy(engine, laid.rearrange("p (c i j) -> p c j i", i=STEP, j=PACK), rows.rearrange("p j (c i) -> p c j i", i=STEP))
 
-        gr, dz2_laid, dz2_q, adj_laid, adj_q = {}, {}, {}, {}, {}
+        factor, dz2_laid, dz2_q, adj_laid, adj_q = {}, {}, {}, {}, {}
 
-        def dz2_scale(g):
-            gr[g] = stage.tile([P, PACK, D_OUT], F32, name="gr", tag="f32", bufs=3)
+        def dz2_factor(g):
+            factor[g] = stage.tile([P, PACK, D_OUT], F32, name="factor", tag="f32", bufs=3)
             for j in range(PACK):
-                nc.scalar.activation(out=gr[g][:, j, :], in_=grad_raw[g][:, j, :], func=COPY, scale=r_sb[:, g, j : j + 1])
+                nc.vector.tensor_scalar(out=factor[g][:, j, :], in0=z2_raw[g][:, j, :], scalar1=0.0, scalar2=r_sb[:, g, j : j + 1], op0=ALU.is_gt, op1=ALU.mult)
 
-        def dz2_mask(g):
+        def dz2_product(g):
             dz2_laid[g] = laid_tile("dz2_laid")
-            nc.vector.scalar_tensor_tensor(
-                out=dz2_laid[g][:].rearrange("p (w j) -> p w j", j=PACK),
-                in0=z2_raw[g][:].rearrange("p j w -> p w j"), scalar=0.0,
-                in1=gr[g][:].rearrange("p j w -> p w j"), op0=ALU.is_gt, op1=ALU.mult)
+            nc.vector.tensor_tensor(
+                out=dz2_laid[g][:].rearrange("p (c i j) -> p c j i", i=STEP, j=PACK),
+                in0=factor[g][:].rearrange("p j (c i) -> p c j i", i=STEP),
+                in1=grad_raw[g][:].rearrange("p j (c i) -> p c j i", i=STEP), op=ALU.mult)
 
         def dz2_quant(g):
             dz2_q[g] = quantize(dz2_laid[g], "dz2", E5M2)
 
         def adj_lay(g, G, engine):
             adj_laid[g, G] = laid_tile("adj_laid")
-            copy(engine, adj_laid[g, G][:].rearrange("p (t q j) -> p t q j", t=PACK, j=PACK), adj_raw[g, G].rearrange("p j (q t) -> p t q j", t=PACK))
+            copy(engine, adj_laid[g, G][:].rearrange("p (t q j) -> p q j t", t=PACK, j=PACK), adj_raw[g, G].rearrange("p j (q t) -> p q j t", t=PACK))
 
         def adj_quant(g, G):
             adj_q[g, G] = quantize(adj_laid[g, G], "adj", E4M3, 8)
@@ -244,20 +243,19 @@ def tile_gcn_v_kernel(tc, inputs, adj, W_kernel, W_bias, r, z2, grad_out, out_0,
             nc.sync.dma_start(out=out_1[P * a : P * (a + 1), :], in_=dw_sb[0][:, a, :])
 
         with tc.manual_schedule():
-            adj_lay(0, 0, "V")
-            adj_lay(1, 0, "V")
-            adj_quant(0, 0)
-            adj_quant(1, 0)
             for g in range(GROUPS):
-                dz2_scale(g)
-                if g > 1:
-                    adj_lay(g, 0, "S")
-                dz2_mask(g)
-                if g > 1:
-                    adj_quant(g, 0)
-                dz2_quant(g)
-                dh_pass(g, 0)
+                adj_lay(g, 0, "S")
+                dz2_factor(g)
+                if g > 0:
+                    dz2_quant(g - 1)
+                dz2_product(g)
+                if g > 0:
+                    adj_quant(g - 1, 0)
+                    dh_pass(g - 1, 0)
+            adj_quant(3, 0)
+            dz2_quant(3)
             adj_lay(0, 1, "S")
+            dh_pass(3, 0)
             w_turn(0)
             w_turn(1)
             for G in range(GROUPS - 1):

@@ -271,52 +271,80 @@ def tile_gcn_v_kernel(tc, inputs, adj, W_kernel, W_bias, r, z2, grad_out, out_0,
                 if G == 0:
                     for b in range(2):
                         w_out(b, "S")
-                if G > 0:
+                elif G == 1:
                     x_lay(G, "S", 0, 256)
+                else:
+                    adj_lay(3, G + 1, "S")
                 adj_lay(2, G + 1, "V")
                 dh_pass(0, G + 1)
                 adj_quant(1, G + 1)
-                dz1_lay(G, "V")
+                if G < 2:
+                    dz1_lay(G, "V")
                 for b in range(2):
                     turn_out(G, b, "S")
-                adj_lay(3, G + 1, "S")
+                if G < 2:
+                    adj_lay(3, G + 1, "S")
                 dh_pass(1, G + 1)
                 if G == 0:
                     w_quant()
+                if G == 1:
+                    x_lay(G, "V", 256, 512)
+                if G == 2:
+                    adj_quant(2, G + 1)
+                    dh_pass(2, G + 1)
+                    adj_quant(3, G + 1)
+                    dz1_lay(2, "V")
                 dz1_quant_f(G)
+                if G == 2:
+                    dh_pass(3, G + 1)
                 for t in range(PACK):
                     dx_pass(G, t)
+                if G == 2:
+                    break
                 if G == 0:
                     x_lay(G, "S", 0, 256)
-                x_lay(G, "V", 256, 512)
-                for g in range(2, PACK):
-                    adj_quant(g, G + 1)
-                    dh_pass(g, G + 1)
+                    x_lay(G, "V", 256, 512)
+                adj_quant(2, G + 1)
+                dh_pass(2, G + 1)
                 dz1_quant_m(G)
+                adj_quant(3, G + 1)
+                dh_pass(3, G + 1)
                 for t in range(PACK):
                     dx_out(G, t, "S")
                 x_quant(G)
-            x_lay(3, "V")
-            x_quant(3)
+            x_lay(2, "S", 0, 256)
+            dx_out(2, 0, "S")
             dz1_tile(3)
             for t in range(PACK):
-                dh_out(3, t, "SSVV"[t])
-            for k in range(2):
-                for a in range(4):
-                    dw_pass(k, a)
+                dh_out(3, t, "SVSV"[t])
             for b in range(2):
                 turn(3, b)
-            for a in range(4):
-                dw_pass(2, a)
-            for b in range(2):
-                turn_out(3, b, "SV"[b])
+            dx_out(2, 1, "S")
+            dz1_quant_m(2)
+            x_lay(2, "V", 256, 512)
+            turn_out(3, 0, "S")
+            turn_out(3, 1, "V")
+            x_quant(2)
             dz1_quant_f(3)
+            dx_out(2, 2, "S")
+            dx_out(2, 3, "S")
+            for a in range(2):
+                for k in range(2):
+                    dw_pass(k, a)
             for t in range(PACK):
                 dx_pass(3, t)
+            for a in range(2, 4):
+                for k in range(2):
+                    dw_pass(k, a)
+            for a in range(4):
+                dw_pass(2, a)
             dz1_lay(3, "V")
+            x_lay(3, "S", 0, 256)
+            x_lay(3, "V", 256, 512)
             dz1_quant_m(3)
+            x_quant(3)
             for t in range(PACK):
-                dx_out(3, t, "S")
+                dx_out(3, t, "SSSV"[t])
             for a in range(4):
                 dw_pass(3, a)
             for a in range(4):

@@ -143,7 +143,7 @@ def tile_gcn_v_kernel(tc, inputs, adj, W_kernel, W_bias, r, z2, grad_out, out_0,
                 nc.tensor.transpose(w_bank[b][:, P * k : P * (k + 1)], words[:, w0 : w0 + 255 : 2], ident[:])
 
         def w_out(b, engine):
-            if b == 0:
+            if "laid" not in w_bank:
                 w_bank["laid"] = laid_tile("w_laid")
             words = w_bank["laid"][:].bitcast(F32)[:, 512 * b : 512 * (b + 1)]
             copy(engine, words.rearrange("p (a f u) -> p a f u", a=2, u=2), w_bank[b][:].rearrange("p (a u f) -> p a f u", a=2, u=2))
@@ -183,7 +183,7 @@ def tile_gcn_v_kernel(tc, inputs, adj, W_kernel, W_bias, r, z2, grad_out, out_0,
                 nc.tensor.transpose(turned[G, b][:, P * k : P * (k + 1)], words[:, w0 : w0 + P], ident[:])
 
         def turn_out(G, b, engine):
-            if b == 0:
+            if G not in dz1_f:
                 dz1_f[G] = laid_tile("dz1_f")
             words = dz1_f[G][:].bitcast(F32)[:, 512 * b : 512 * (b + 1)]
             copy(engine, words.rearrange("p (t m u) -> p t m u", t=2, u=2), turned[G, b][:].rearrange("p (t u m) -> p t m u", t=2, u=2))
@@ -208,7 +208,7 @@ def tile_gcn_v_kernel(tc, inputs, adj, W_kernel, W_bias, r, z2, grad_out, out_0,
                 rhs=w_q[0][:].bitcast(E4M3), rhs_scale=w_q[1][:], start=True, stop=True)
 
         def dx_out(G, t, engine):
-            if t == 0:
+            if G not in dx_sb:
                 dx_sb[G] = stage.tile([P, PACK, F_IN], F32, name="dx_sb", tag="f32", bufs=3)
             copy(engine, dx_sb[G][:, t, :], dx[G, t][:])
             if G == GROUPS - 1:
@@ -219,7 +219,7 @@ def tile_gcn_v_kernel(tc, inputs, adj, W_kernel, W_bias, r, z2, grad_out, out_0,
         x_laid, x_q = {}, {}
 
         def x_lay(G, engine, c0=0, c1=F_IN):
-            if c0 == 0:
+            if G not in x_laid:
                 x_laid[G] = laid_tile("x_laid")
             lay_rows(engine, x_raw[G][:, :, c0:c1], x_laid[G][:, PACK * c0 : PACK * c1])
 
@@ -237,115 +237,186 @@ def tile_gcn_v_kernel(tc, inputs, adj, W_kernel, W_bias, r, z2, grad_out, out_0,
                 rhs=dz1_mq[G][0][:].bitcast(E5M2), rhs_scale=dz1_mq[G][1][:], start=(G == 0), stop=(G == GROUPS - 1))
 
         def dw_out(a, engine):
-            if a == 0:
+            if not dw_sb:
                 dw_sb[0] = stage.tile([P, F_IN // P, D_OUT], F32, name="dw_sb", tag="f32", bufs=3)
             copy(engine, dw_sb[0][:, a, :].rearrange("p (q u e) -> p q u e", u=2, e=2), dw[a][:].rearrange("p (u q e) -> p q u e", u=2, e=2))
             nc.sync.dma_start(out=out_1[P * a : P * (a + 1), :], in_=dw_sb[0][:, a, :])
 
         with tc.manual_schedule():
-            for g in range(GROUPS):
-                adj_lay(g, 0, "S")
-                dz2_factor(g)
-                if g > 0:
-                    dz2_quant(g - 1)
-                dz2_product(g)
-                if g > 0:
-                    adj_quant(g - 1, 0)
-                    dh_pass(g - 1, 0)
+            adj_lay(0, 0, "S")
+            dz2_factor(0)
+            dz2_product(0)
+            dz2_quant(0)
+            adj_quant(0, 0)
+            dz2_factor(1)
+            adj_lay(1, 0, "S")
+            dz2_product(1)
+            dz2_factor(2)
+            dz2_quant(1)
+            dz2_product(2)
+            adj_quant(1, 0)
+            adj_lay(2, 0, "S")
+            dz2_quant(2)
+            dz2_factor(3)
+            adj_quant(2, 0)
+            dh_pass(0, 0)
+            dz2_product(3)
+            dh_pass(1, 0)
+            dh_pass(2, 0)
+            adj_lay(3, 0, "S")
             adj_quant(3, 0)
             dz2_quant(3)
-            adj_lay(0, 1, "S")
             dh_pass(3, 0)
             w_turn(0)
             w_turn(1)
-            for G in range(GROUPS - 1):
-                dz1_tile(G)
-                for t in range(PACK):
-                    dh_out(G, t, "S")
-                if G > 0:
-                    adj_lay(0, G + 1, "V")
-                adj_lay(1, G + 1, "V")
-                adj_quant(0, G + 1)
-                for b in range(2):
-                    turn(G, b)
-                if G == 0:
-                    for b in range(2):
-                        w_out(b, "S")
-                elif G == 1:
-                    x_lay(G, "S", 0, 256)
-                else:
-                    adj_lay(3, G + 1, "S")
-                adj_lay(2, G + 1, "V")
-                dh_pass(0, G + 1)
-                adj_quant(1, G + 1)
-                if G < 2:
-                    dz1_lay(G, "V")
-                for b in range(2):
-                    turn_out(G, b, "S")
-                if G < 2:
-                    adj_lay(3, G + 1, "S")
-                dh_pass(1, G + 1)
-                if G == 0:
-                    w_quant()
-                if G == 1:
-                    x_lay(G, "V", 256, 512)
-                if G == 2:
-                    adj_quant(2, G + 1)
-                    dh_pass(2, G + 1)
-                    adj_quant(3, G + 1)
-                    dz1_lay(2, "V")
-                dz1_quant_f(G)
-                if G == 2:
-                    dh_pass(3, G + 1)
-                for t in range(PACK):
-                    dx_pass(G, t)
-                if G == 2:
-                    break
-                if G == 0:
-                    x_lay(G, "S", 0, 256)
-                    x_lay(G, "V", 256, 512)
-                adj_quant(2, G + 1)
-                dh_pass(2, G + 1)
-                dz1_quant_m(G)
-                adj_quant(3, G + 1)
-                dh_pass(3, G + 1)
-                for t in range(PACK):
-                    dx_out(G, t, "S")
-                x_quant(G)
-            x_lay(2, "S", 0, 256)
-            dx_out(2, 0, "S")
+            adj_lay(1, 1, "V")
+            adj_lay(0, 1, "S")
+            adj_lay(2, 1, "V")
+            dz1_tile(0)
+            dh_out(0, 0, "S")
+            dh_out(0, 1, "S")
+            adj_quant(0, 1)
+            dh_out(0, 2, "S")
+            dh_out(0, 3, "S")
+            adj_quant(1, 1)
+            w_out(0, "S")
+            w_out(1, "S")
+            turn(0, 0)
+            turn(0, 1)
+            adj_lay(3, 1, "V")
+            w_quant()
+            x_lay(0, "S", 0, 256)
+            adj_quant(2, 1)
+            dh_pass(0, 1)
+            x_lay(0, "V", 256, 512)
+            dh_pass(1, 1)
+            adj_quant(3, 1)
+            adj_lay(0, 2, "V")
+            dh_pass(2, 1)
+            turn_out(0, 0, "S")
+            turn_out(0, 1, "S")
+            dz1_quant_f(0)
+            dh_pass(3, 1)
+            adj_lay(1, 2, "V")
+            dx_pass(0, 2)
+            dx_pass(0, 3)
+            dz1_lay(0, "S")
+            dz1_tile(1)
+            dh_out(1, 0, "S")
+            dh_out(1, 1, "V")
+            dx_pass(0, 0)
+            dx_pass(0, 1)
+            dh_out(1, 2, "S")
+            dh_out(1, 3, "S")
+            dx_out(0, 2, "S")
+            dx_out(0, 3, "S")
+            dx_out(0, 0, "S")
+            dx_out(0, 1, "S")
+            adj_quant(0, 2)
+            adj_quant(1, 2)
+            turn(1, 0)
+            turn(1, 1)
+            dh_pass(0, 2)
+            adj_lay(2, 2, "V")
+            turn_out(1, 0, "S")
+            turn_out(1, 1, "S")
+            adj_lay(0, 3, "V")
+            dz1_quant_f(1)
+            x_quant(0)
+            adj_quant(2, 2)
+            dh_pass(1, 2)
+            dx_pass(1, 2)
+            dx_pass(1, 3)
+            dx_pass(1, 0)
+            dx_pass(1, 1)
+            adj_lay(1, 3, "V")
+            adj_lay(3, 2, "S")
+            dx_out(1, 0, "S")
+            dx_out(1, 1, "S")
+            adj_quant(3, 2)
+            dx_out(1, 2, "S")
+            dx_out(1, 3, "S")
+            adj_quant(1, 3)
+            dh_pass(2, 2)
+            dh_pass(3, 2)
+            dz1_tile(2)
+            dh_out(2, 0, "S")
+            dh_out(2, 1, "S")
+            adj_quant(0, 3)
+            adj_lay(2, 3, "V")
+            dh_out(2, 2, "S")
+            dh_out(2, 3, "S")
+            dh_pass(0, 3)
+            dz1_quant_m(0)
+            adj_lay(3, 3, "V")
+            turn(2, 0)
+            turn(2, 1)
+            dh_pass(1, 3)
+            adj_quant(2, 3)
+            dz1_lay(1, "V")
+            x_lay(1, "S", 256, 512)
+            turn_out(2, 0, "S")
+            turn_out(2, 1, "S")
+            dh_pass(2, 3)
+            adj_quant(3, 3)
+            x_lay(1, "V", 0, 256)
+            dh_pass(3, 3)
+            dz1_lay(2, "S")
+            dz1_quant_f(2)
+            dz1_quant_m(1)
             dz1_tile(3)
-            for t in range(PACK):
-                dh_out(3, t, "SVSV"[t])
-            for b in range(2):
-                turn(3, b)
-            dx_out(2, 1, "S")
+            dh_out(3, 0, "S")
+            dh_out(3, 1, "S")
+            dx_pass(2, 0)
+            dx_pass(2, 1)
             dz1_quant_m(2)
+            dh_out(3, 2, "S")
+            dh_out(3, 3, "S")
+            dx_out(2, 0, "V")
+            dx_out(2, 1, "S")
             x_lay(2, "V", 256, 512)
-            turn_out(3, 0, "S")
+            dx_pass(2, 2)
+            dx_pass(2, 3)
+            turn(3, 0)
+            turn(3, 1)
+            x_quant(1)
+            turn_out(3, 0, "V")
             turn_out(3, 1, "V")
-            x_quant(2)
-            dz1_quant_f(3)
+            x_lay(2, "V", 0, 256)
             dx_out(2, 2, "S")
             dx_out(2, 3, "S")
-            for a in range(2):
-                for k in range(2):
-                    dw_pass(k, a)
-            for t in range(PACK):
-                dx_pass(3, t)
-            for a in range(2, 4):
-                for k in range(2):
-                    dw_pass(k, a)
-            for a in range(4):
-                dw_pass(2, a)
-            dz1_lay(3, "V")
-            x_lay(3, "S", 0, 256)
+            dw_pass(0, 0)
+            dw_pass(0, 1)
+            dw_pass(0, 2)
+            dw_pass(0, 3)
+            dw_pass(1, 0)
+            dw_pass(1, 1)
+            dw_pass(1, 2)
+            dw_pass(1, 3)
+            dz1_quant_f(3)
             x_lay(3, "V", 256, 512)
-            dz1_quant_m(3)
+            x_lay(3, "V", 0, 256)
+            dx_pass(3, 0)
+            dx_pass(3, 1)
+            x_quant(2)
+            dx_pass(3, 2)
+            dx_pass(3, 3)
+            dz1_lay(3, "S")
             x_quant(3)
-            for t in range(PACK):
-                dx_out(3, t, "SSSV"[t])
-            for a in range(4):
-                dw_pass(3, a)
-            for a in range(4):
-                dw_out(a, "VS"[a % 2])
+            dw_pass(2, 0)
+            dw_pass(2, 1)
+            dw_pass(2, 2)
+            dw_pass(2, 3)
+            dx_out(3, 0, "S")
+            dx_out(3, 1, "S")
+            dz1_quant_m(3)
+            dx_out(3, 2, "S")
+            dx_out(3, 3, "S")
+            dw_pass(3, 0)
+            dw_pass(3, 1)
+            dw_pass(3, 2)
+            dw_pass(3, 3)
+            dw_out(0, "V")
+            dw_out(1, "S")
+            dw_out(2, "S")
+            dw_out(3, "V")

from contextlib import ExitStack

import concourse.mybir as mybir
from concourse.masks import make_identity

NODES, F_IN, D_OUT = 2048, 512, 512
FLOPS = 2 * NODES * NODES * D_OUT + 2 * 2 * NODES * F_IN * D_OUT
BYTES = 2 * (NODES * F_IN + NODES * NODES + F_IN * D_OUT + NODES * D_OUT) + 4 * (NODES + NODES * D_OUT) + 4 * (NODES * F_IN + F_IN * D_OUT)

F32 = mybir.dt.float32
BF16 = mybir.dt.bfloat16
U32 = mybir.dt.uint32
U8 = mybir.dt.uint8
E4M3 = mybir.dt.float8_e4m3fn_x4
E5M2 = mybir.dt.float8_e5m2_x4
ALU = mybir.AluOpType
COPY = mybir.ActivationFunctionType.Copy

P = 128
PACK = 4
GROUP = P * PACK
GROUPS = NODES // GROUP
HALF = NODES // 2
STEP = 4


def tile_gcn_v_kernel(tc, inputs, adj, W_kernel, W_bias, r, z2, grad_out, out_0, out_1):
    nc = tc.nc
    x_rows = inputs.rearrange("o (g p j) f -> g p (o j) f", g=GROUPS, j=PACK)
    adj_rows = adj.rearrange("o (g p j) m -> g p (o j) m", g=GROUPS, j=PACK)
    z2_rows = z2.rearrange("o (g p j) w -> g p (o j) w", g=GROUPS, j=PACK)
    grad_rows = grad_out.rearrange("o (g p j) w -> g p (o j) w", g=GROUPS, j=PACK)
    r_cols = r.rearrange("o (g p j) -> p (o g) j", g=GROUPS, j=PACK)
    w_rows = W_kernel.rearrange("(a p) j -> p a j", p=P)
    dx_rows = out_0.rearrange("o (g p j) f -> g p (o j) f", g=GROUPS, j=PACK)

    with ExitStack() as ctx:
        keep = ctx.enter_context(tc.tile_pool(name="keep", bufs=1))
        codes = ctx.enter_context(tc.tile_pool(name="codes", bufs=1))
        stage = ctx.enter_context(tc.tile_pool(name="stage", bufs=3))
        psum = ctx.enter_context(tc.psum_pool(name="psum", bufs=1))

        def bank(i):
            return psum.tile([P, 512], F32, name=f"bank{i}")

        def operand(name, bufs):
            return (codes.tile([P, GROUP], U32, name=f"{name}_codes", bufs=bufs, align_bytes=64),
                    codes.tile([P, GROUP], U8, name=f"{name}_scales", bufs=bufs, align_bytes=64))

        ident = keep.tile([P, P], F32, name="ident")
        make_identity(nc, ident[:])
        r_sb = keep.tile([P, GROUPS, PACK], F32, name="r_sb")
        nc.scalar.dma_start(out=r_sb[:], in_=r_cols)
        adj_raw, z2_raw, grad_raw, x_raw = {}, {}, {}, {}

        def load_z2(g):
            z2_raw[g] = stage.tile([P, PACK, D_OUT], F32, name="z2_raw")
            nc.sync.dma_start(out=z2_raw[g][:], in_=z2_rows[g])

        def load_grad(g):
            grad_raw[g] = stage.tile([P, PACK, D_OUT], BF16, name="grad_raw", tag="rows", bufs=4)
            nc.sync.dma_start(out=grad_raw[g][:], in_=grad_rows[g])

        def load_adj(g, G, width):
            raw = stage.tile([P, PACK, width * GROUP], BF16, name=f"adj_raw{width}", bufs=6 if width == 1 else 4)
            nc.sync.dma_start(out=raw[:], in_=adj_rows[g][:, :, G * GROUP : (G + width) * GROUP])
            for k in range(width):
                adj_raw[g, G + k] = raw[:, :, k * GROUP : (k + 1) * GROUP]

        def load_x(g):
            x_raw[g] = stage.tile([P, PACK, F_IN], BF16, name="x_raw", tag="rows", bufs=4)
            nc.sync.dma_start(out=x_raw[g][:], in_=x_rows[g])

        for g in range(GROUPS):
            load_z2(g)
            if g < 3:
                load_grad(g)
            load_adj(g, 0, 1)
        load_grad(3)
        load_adj(0, 1, 1)
        load_adj(1, 1, 1)
        w_raw = keep.tile([P, 4, D_OUT], BF16, name="w_raw")
        nc.sync.dma_start(out=w_raw[:], in_=w_rows)
        load_adj(2, 1, 1)
        load_adj(3, 1, 1)
        load_x(0)
        load_adj(0, 2, 2)
        load_adj(1, 2, 2)
        load_x(1)
        load_adj(2, 2, 2)
        load_adj(3, 2, 2)
        load_x(2)
        load_x(3)

        def copy(engine, out, in_):
            if engine == "V":
                nc.vector.tensor_copy(out=out, in_=in_)
            else:
                nc.scalar.copy(out=out, in_=in_)

        def quantize(laid, name, fmt, bufs=4):
            words, scales = operand(name, bufs)
            nc.vector.quantize_mx(out=words[:].bitcast(fmt), scales=scales[:], in_=laid[:])
            return words, scales

        def laid_tile(name):
            return stage.tile([P, GROUP * PACK], BF16, name=name, tag="laid", bufs=8, align_bytes=64)

        def lay_rows(engine, rows, laid):
            copy(engine, laid.rearrange("p (c i j) -> p c j i", i=STEP, j=PACK), rows.rearrange("p j (c i) -> p c j i", i=STEP))

        factor, dz2_laid, dz2_q, adj_laid, adj_q = {}, {}, {}, {}, {}

        def dz2_factor(g):
            factor[g] = stage.tile([P, PACK, D_OUT], F32, name="factor", tag="f32", bufs=3)
            for j in range(PACK):
                nc.vector.tensor_scalar(out=factor[g][:, j, :], in0=z2_raw[g][:, j, :], scalar1=0.0, scalar2=r_sb[:, g, j : j + 1], op0=ALU.is_gt, op1=ALU.mult)

        def dz2_product(g):
            dz2_laid[g] = laid_tile("dz2_laid")
            nc.vector.tensor_tensor(
                out=dz2_laid[g][:].rearrange("p (c i j) -> p c j i", i=STEP, j=PACK),
                in0=factor[g][:].rearrange("p j (c i) -> p c j i", i=STEP),
                in1=grad_raw[g][:].rearrange("p j (c i) -> p c j i", i=STEP), op=ALU.mult)

        def dz2_quant(g):
            dz2_q[g] = quantize(dz2_laid[g], "dz2", E5M2)

        def adj_lay(g, G, engine):
            adj_laid[g, G] = laid_tile("adj_laid")
            copy(engine, adj_laid[g, G][:].rearrange("p (t q j) -> p q j t", t=PACK, j=PACK), adj_raw[g, G].rearrange("p j (q t) -> p q j t", t=PACK))

        def adj_quant(g, G):
            adj_q[g, G] = quantize(adj_laid[g, G], "adj", E4M3, 8)

        w_bank, w_q = {}, {}

        def w_turn(b):
            words = w_raw[:].rearrange("p a w -> p (a w)").bitcast(F32)
            w_bank[b] = bank(4 + b)
            for k in range(4):
                w0 = 512 * b + 256 * (k // 2) + k % 2
                nc.tensor.transpose(w_bank[b][:, P * k : P * (k + 1)], words[:, w0 : w0 + 255 : 2], ident[:])

        def w_out(b, engine):
            if "laid" not in w_bank:
                w_bank["laid"] = laid_tile("w_laid")
            words = w_bank["laid"][:].bitcast(F32)[:, 512 * b : 512 * (b + 1)]
            copy(engine, words.rearrange("p (a f u) -> p a f u", a=2, u=2), w_bank[b][:].rearrange("p (a u f) -> p a f u", a=2, u=2))

        def w_quant():
            w_q[0], w_q[1] = quantize(w_bank["laid"], "w", E4M3, 1)

        dh = {}

        def dh_pass(g, G):
            for t in range(PACK):
                if g == 0:
                    dh[G, t] = bank(4 * (G % 2) + t)
                cols = slice(P * t, P * (t + 1))
                nc.tensor.matmul_mx(
                    out=dh[G, t][:], lhsT=adj_q[g, G][0][:, cols].bitcast(E4M3), lhsT_scale=adj_q[g, G][1][:, cols],
                    rhs=dz2_q[g][0][:].bitcast(E5M2), rhs_scale=dz2_q[g][1][:], start=(g == 0), stop=(g == GROUPS - 1))

        dz1, dz1_f, dz1_laid, dz1_fq, dz1_mq, turned = {}, {}, {}, {}, {}, {}

        def dz1_tile(G):
            dz1[G] = stage.tile([P, PACK, D_OUT], BF16, name="dz1", bufs=2)

        def dh_out(G, t, engine):
            out = dz1[G][:, t, :].rearrange("p (u q e) -> p u q e", u=2, e=2)
            in_ = dh[G, t][:].rearrange("p (q u e) -> p u q e", u=2, e=2)
            if engine == "V":
                nc.vector.tensor_scalar(out=out, in0=in_, scalar1=r_sb[:, G, t : t + 1], scalar2=None, op0=ALU.mult)
            else:
                nc.scalar.activation(out=out, in_=in_, func=COPY, scale=r_sb[:, G, t : t + 1])

        def turn(G, b):
            words = dz1[G][:].rearrange("p t w -> p (t w)").bitcast(F32)
            turned[G, b] = bank(4 * (G % 2) + b)
            for k in range(4):
                w0 = 512 * b + P * k
                nc.tensor.transpose(turned[G, b][:, P * k : P * (k + 1)], words[:, w0 : w0 + P], ident[:])

        def turn_out(G, b, engine):
            if G not in dz1_f:
                dz1_f[G] = laid_tile("dz1_f")
            words = dz1_f[G][:].bitcast(F32)[:, 512 * b : 512 * (b + 1)]
            copy(engine, words.rearrange("p (t m u) -> p t m u", t=2, u=2), turned[G, b][:].rearrange("p (t u m) -> p t m u", t=2, u=2))

        def dz1_lay(G, engine):
            dz1_laid[G] = laid_tile("dz1_laid")
            lay_rows(engine, dz1[G][:], dz1_laid[G][:])

        def dz1_quant_f(G):
            dz1_fq[G] = quantize(dz1_f[G], "dz1_f", E5M2, 2)

        def dz1_quant_m(G):
            dz1_mq[G] = quantize(dz1_laid[G], "dz1_m", E5M2)

        dx, dx_sb = {}, {}

        def dx_pass(G, t):
            dx[G, t] = bank(4 * (G % 2) + (2 + t) % 4)
            cols = slice(P * t, P * (t + 1))
            nc.tensor.matmul_mx(
                out=dx[G, t][:], lhsT=dz1_fq[G][0][:, cols].bitcast(E5M2), lhsT_scale=dz1_fq[G][1][:, cols],
                rhs=w_q[0][:].bitcast(E4M3), rhs_scale=w_q[1][:], start=True, stop=True)

        def dx_out(G, t, engine):
            if G not in dx_sb:
                dx_sb[G] = stage.tile([P, PACK, F_IN], F32, name="dx_sb", tag="f32", bufs=3)
            copy(engine, dx_sb[G][:, t, :], dx[G, t][:])
            if G == GROUPS - 1:
                nc.sync.dma_start(out=dx_rows[G][:, t, :], in_=dx_sb[G][:, t, :])
            elif t % 2 == 1:
                nc.sync.dma_start(out=dx_rows[G][:, t - 1 : t + 1, :], in_=dx_sb[G][:, t - 1 : t + 1, :])

        x_laid, x_q = {}, {}

        def x_lay(G, engine, c0=0, c1=F_IN):
            if G not in x_laid:
                x_laid[G] = laid_tile("x_laid")
            lay_rows(engine, x_raw[G][:, :, c0:c1], x_laid[G][:, PACK * c0 : PACK * c1])

        def x_quant(G):
            x_q[G] = quantize(x_laid[G], "x", E4M3)

        dw, dw_sb = {}, {}

        def dw_pass(G, a):
            if G == 0:
                dw[a] = bank((2 + a) % 4)
            cols = slice(P * a, P * (a + 1))
            nc.tensor.matmul_mx(
                out=dw[a][:], lhsT=x_q[G][0][:, cols].bitcast(E4M3), lhsT_scale=x_q[G][1][:, cols],
                rhs=dz1_mq[G][0][:].bitcast(E5M2), rhs_scale=dz1_mq[G][1][:], start=(G == 0), stop=(G == GROUPS - 1))

        def dw_out(a, engine):
            if not dw_sb:
                dw_sb[0] = stage.tile([P, F_IN // P, D_OUT], F32, name="dw_sb", tag="f32", bufs=3)
            copy(engine, dw_sb[0][:, a, :].rearrange("p (q u e) -> p q u e", u=2, e=2), dw[a][:].rearrange("p (u q e) -> p q u e", u=2, e=2))
            nc.sync.dma_start(out=out_1[P * a : P * (a + 1), :], in_=dw_sb[0][:, a, :])

        with tc.manual_schedule():
            adj_lay(0, 0, "S")
            dz2_factor(0)
            dz2_product(0)
            dz2_quant(0)
            adj_quant(0, 0)
            dz2_factor(1)
            adj_lay(1, 0, "S")
            dz2_product(1)
            dz2_factor(2)
            dz2_quant(1)
            dz2_product(2)
            adj_quant(1, 0)
            adj_lay(2, 0, "S")
            dz2_quant(2)
            dz2_factor(3)
            adj_quant(2, 0)
            dh_pass(0, 0)
            dz2_product(3)
            dh_pass(1, 0)
            dh_pass(2, 0)
            adj_lay(3, 0, "S")
            adj_quant(3, 0)
            dz2_quant(3)
            dh_pass(3, 0)
            w_turn(0)
            w_turn(1)
            adj_lay(1, 1, "V")
            adj_lay(0, 1, "S")
            adj_lay(2, 1, "V")
            dz1_tile(0)
            dh_out(0, 0, "S")
            dh_out(0, 1, "S")
            adj_quant(0, 1)
            dh_out(0, 2, "S")
            dh_out(0, 3, "S")
            adj_quant(1, 1)
            w_out(0, "S")
            w_out(1, "S")
            turn(0, 0)
            turn(0, 1)
            adj_lay(3, 1, "V")
            w_quant()
            x_lay(0, "S", 0, 256)
            adj_quant(2, 1)
            dh_pass(0, 1)
            x_lay(0, "V", 256, 512)
            dh_pass(1, 1)
            adj_quant(3, 1)
            adj_lay(0, 2, "V")
            dh_pass(2, 1)
            turn_out(0, 0, "S")
            turn_out(0, 1, "S")
            dz1_quant_f(0)
            dh_pass(3, 1)
            adj_lay(1, 2, "V")
            dx_pass(0, 2)
            dx_pass(0, 3)
            dz1_lay(0, "S")
            dz1_tile(1)
            dh_out(1, 0, "S")
            dh_out(1, 1, "V")
            dx_pass(0, 0)
            dx_pass(0, 1)
            dh_out(1, 2, "S")
            dh_out(1, 3, "S")
            dx_out(0, 2, "S")
            dx_out(0, 3, "S")
            dx_out(0, 0, "S")
            dx_out(0, 1, "S")
            adj_quant(0, 2)
            adj_quant(1, 2)
            turn(1, 0)
            turn(1, 1)
            dh_pass(0, 2)
            adj_lay(2, 2, "V")
            turn_out(1, 0, "S")
            turn_out(1, 1, "S")
            adj_lay(0, 3, "V")
            dz1_quant_f(1)
            x_quant(0)
            adj_quant(2, 2)
            dh_pass(1, 2)
            dx_pass(1, 2)
            dx_pass(1, 3)
            dx_pass(1, 0)
            dx_pass(1, 1)
            adj_lay(1, 3, "V")
            adj_lay(3, 2, "S")
            dx_out(1, 0, "S")
            dx_out(1, 1, "S")
            adj_quant(3, 2)
            dx_out(1, 2, "S")
            dx_out(1, 3, "S")
            adj_quant(1, 3)
            dh_pass(2, 2)
            dh_pass(3, 2)
            dz1_tile(2)
            dh_out(2, 0, "S")
            dh_out(2, 1, "S")
            adj_quant(0, 3)
            adj_lay(2, 3, "V")
            dh_out(2, 2, "S")
            dh_out(2, 3, "S")
            dh_pass(0, 3)
            dz1_quant_m(0)
            adj_lay(3, 3, "V")
            turn(2, 0)
            turn(2, 1)
            dh_pass(1, 3)
            adj_quant(2, 3)
            dz1_lay(1, "V")
            x_lay(1, "S", 256, 512)
            turn_out(2, 0, "S")
            turn_out(2, 1, "S")
            dh_pass(2, 3)
            adj_quant(3, 3)
            x_lay(1, "V", 0, 256)
            dh_pass(3, 3)
            dz1_lay(2, "S")
            dz1_quant_f(2)
            dz1_quant_m(1)
            dz1_tile(3)
            dh_out(3, 0, "S")
            dh_out(3, 1, "S")
            dx_pass(2, 0)
            dx_pass(2, 1)
            dz1_quant_m(2)
            dh_out(3, 2, "S")
            dh_out(3, 3, "S")
            dx_out(2, 0, "V")
            dx_out(2, 1, "S")
            x_lay(2, "V", 256, 512)
            dx_pass(2, 2)
            dx_pass(2, 3)
            turn(3, 0)
            turn(3, 1)
            x_quant(1)
            turn_out(3, 0, "V")
            turn_out(3, 1, "V")
            x_lay(2, "V", 0, 256)
            dx_out(2, 2, "S")
            dx_out(2, 3, "S")
            dw_pass(0, 0)
            dw_pass(0, 1)
            dw_pass(0, 2)
            dw_pass(0, 3)
            dw_pass(1, 0)
            dw_pass(1, 1)
            dw_pass(1, 2)
            dw_pass(1, 3)
            dz1_quant_f(3)
            x_lay(3, "V", 256, 512)
            x_lay(3, "V", 0, 256)
            dx_pass(3, 0)
            dx_pass(3, 1)
            x_quant(2)
            dx_pass(3, 2)
            dx_pass(3, 3)
            dz1_lay(3, "S")
            x_quant(3)
            dw_pass(2, 0)
            dw_pass(2, 1)
            dw_pass(2, 2)
            dw_pass(2, 3)
            dx_out(3, 0, "S")
            dx_out(3, 1, "S")
            dz1_quant_m(3)
            dx_out(3, 2, "S")
            dx_out(3, 3, "S")
            dw_pass(3, 0)
            dw_pass(3, 1)
            dw_pass(3, 2)
            dw_pass(3, 3)
            dw_out(0, "V")
            dw_out(1, "S")
            dw_out(2, "S")
            dw_out(3, "V")
